import numpy as np
import ml_dtypes


def mxq(x, axis, fmt="e4m3"):
    dtype, down = {"e4m3": (ml_dtypes.float8_e4m3fn, 7), "e5m2": (ml_dtypes.float8_e5m2, 14)}[fmt]
    v = np.moveaxis(np.asarray(x, np.float32).astype(ml_dtypes.bfloat16).astype(np.float64), axis, -1)
    blocks = v.reshape(v.shape[:-1] + (-1, 32))
    amax = np.abs(blocks).max(-1, keepdims=True)
    byte = np.maximum(np.where(amax > 0, np.frexp(amax)[1] - 1 + 127, 0) - down, 1)
    scale = np.exp2(byte - 127.0)
    codes = (blocks / scale).astype(np.float32).astype(dtype).astype(np.float64)
    return np.moveaxis((codes * scale).reshape(v.shape), -1, axis)


WIDE = False


def mx_kscale(k):
    if not WIDE:
        return np.ones(k)
    levels = np.array([10, -10, 5, -5, 0])
    if k % 512:
        return np.exp2(np.random.permutation(np.resize(levels, k // 32))).repeat(32)
    a = np.empty((k // 512, 16))
    for p in range(k // 512):
        a[p, :8] = np.random.permutation(np.resize(levels, 8))
        for g in range(8):
            far = levels[np.abs(levels - a[p, g]) >= 10]
            a[p, g + 8] = far[np.random.randint(len(far))]
    return np.exp2(a.ravel()).repeat(32)


BF16 = ml_dtypes.bfloat16


def bf(x):
    return np.asarray(x, np.float32).astype(BF16)


def f64(x):
    return np.asarray(x).astype(np.float64)


B, C, NB, BW, T, EMB = 4, 2, 8, 128, 512, 128
F = NB * BW
FEAT = C * BW * 2
EPS = 1e-5


def setup_inputs():
    s = mx_kscale(FEAT)
    amp = np.exp2(np.random.uniform(-9.0, 1.0, (B, 1, 1, T)))
    return {"x_real": bf(amp * (np.random.standard_normal((B, C, F, T)) + 0.6)),
            "x_imag": bf(amp * (np.random.standard_normal((B, C, F, T)) + 0.2)),
            "ln_w": bf((1.0 + 0.1 * np.random.standard_normal((NB, FEAT))) * s),
            "ln_b": bf(0.1 * np.random.standard_normal((NB, FEAT)) * s),
            "fc_w": bf(np.random.standard_normal((NB, FEAT, EMB)) / np.sqrt(FEAT) / s[:, None]),
            "fc_b": bf(0.3 * np.random.standard_normal((NB, EMB)))}


def reference(x_real, x_imag, ln_w, ln_b, fc_w, fc_b):
    x_real, x_imag, ln_w, ln_b, fc_w, fc_b = f64(x_real), f64(x_imag), f64(ln_w), f64(ln_b), f64(fc_w), f64(fc_b)
    b, c, f, t = x_real.shape
    nb, feat = ln_w.shape
    bw = f // nb
    xr = np.transpose(x_real, (0, 3, 1, 2)).reshape(b, t, c, nb, bw)
    xi = np.transpose(x_imag, (0, 3, 1, 2)).reshape(b, t, c, nb, bw)
    xb = np.stack([xr, xi], axis=-1)
    xb = np.transpose(xb, (0, 3, 1, 2, 4, 5))
    xb = xb.reshape(b, nb, t, feat)
    mean = np.mean(xb, axis=-1, keepdims=True)
    var = np.mean(np.square(xb - mean), axis=-1, keepdims=True)
    xn = (xb - mean) * (1.0 / np.sqrt(var + EPS))
    xn = xn * ln_w[None, :, None, :] + ln_b[None, :, None, :]
    z = (mxq(xn, 3, "e4m3") @ mxq(fc_w, 1, "e4m3")[None]) + fc_b[None, :, None, :]
    return z

@@ -1,0 +1,293 @@
+from contextlib import ExitStack
+
+import concourse.mybir as mybir
+from concourse.masks import make_identity
+
+F32 = mybir.dt.float32
+BF16 = mybir.dt.bfloat16
+U32 = mybir.dt.uint32
+U8 = mybir.dt.uint8
+FP8X4 = mybir.dt.float8_e4m3fn_x4
+ACT = mybir.ActivationFunctionType
+ALU = mybir.AluOpType
+
+B, C, NB, BW, T, EMB = 4, 2, 8, 128, 512, 128
+P = 128
+SLOTS = 4
+PAIRS = BW // 2
+EPS = 1e-5
+FLOPS = 2 * B * NB * T * (SLOTS * BW) * EMB
+GB = 4
+UNITS = B * NB
+GROUPS = UNITS // GB
+WHOLE = ((0, GB),)
+
+
+def tile_bandsplitmodule_kernel(tc, x_real, x_imag, ln_w, ln_b, fc_w, fc_b, out):
+    nc = tc.nc
+    with ExitStack() as ctx:
+        const = ctx.enter_context(tc.tile_pool(name="const", bufs=1))
+        xpool = ctx.enter_context(tc.tile_pool(name="xpool", bufs=4))
+        work = ctx.enter_context(tc.tile_pool(name="work", bufs=3))
+        small = ctx.enter_context(tc.tile_pool(name="small", bufs=8))
+        psx = ctx.enter_context(tc.psum_pool(name="psx", bufs=4))
+        psy = ctx.enter_context(tc.psum_pool(name="psy", bufs=3))
+        psz = ctx.enter_context(tc.psum_pool(name="psz", bufs=1))
+        ctx.enter_context(tc.manual_schedule())
+
+        xs, xts, mvs, sds, rstds, nmrs, ys, yts, xnps, grps, zos = {}, {}, {}, {}, {}, {}, {}, {}, {}, {}, {}
+        wq, cds, sts = {}, {}, {}
+
+        def load(grp_i, cuts):
+            b, g = grp_i // 2, grp_i % 2
+            xin = xpool.tile([P, 2, GB, 2 * T], BF16, name="xin")
+            for lo, hi in cuts:
+                for r, src in enumerate((x_real, x_imag)):
+                    for c in range(C):
+                        nc.sync.dma_start(
+                            out=xin[PAIRS * c : PAIRS * c + PAIRS, r, lo:hi, :],
+                            in_=src[b, c].rearrange("(n j i) t -> j n (i t)", j=PAIRS, i=2)[:, GB * g + lo : GB * g + hi, :],
+                        )
+            xs[grp_i] = xin
+
+        ident = const.tile([P, P], F32)
+        make_identity(nc, ident[:])
+        zero1 = const.tile([P, 1], F32)
+        nc.vector.memset(zero1[:], 0.0)
+        eps = const.tile([P, 1], F32)
+        nc.vector.tensor_scalar(out=eps[:], in0=zero1[:], scalar1=EPS, scalar2=None, op0=ALU.add)
+
+        lnraw = const.tile([P, SLOTS * BW], BF16)
+        nc.vector.memset(lnraw[:], 0.0)
+        nc.scalar.dma_start(out=lnraw[0:NB, :], in_=ln_w)
+        nc.scalar.dma_start(out=lnraw[NB : 2 * NB, :], in_=ln_b)
+        load(0, ((0, 1), (1, GB)))
+        wraw = const.tile([P, NB, SLOTS, EMB], BF16)
+        nc.sync.dma_start(
+            out=wraw[:].rearrange("p n s e -> p n (s e)"),
+            in_=fc_w.rearrange("n (p s) e -> p n (s e)", s=SLOTS),
+        )
+        load(1, WHOLE)
+        fcb = const.tile([P, NB * EMB], BF16)
+        nc.sync.dma_start(out=fcb[:], in_=fc_b.rearrange("n e -> (n e)").partition_broadcast(P))
+        load(2, WHOLE)
+
+        lnt = psx.tile([P, SLOTS, P], F32, tag="xt")
+        lnwords = lnraw[:].bitcast(F32)
+        for u in range(2):
+            nc.tensor.transpose(lnt[:, u, :], lnwords[:, u::2], ident[:])
+        lnv = lnt[:].bitcast(BF16)
+        lnw = const.tile([P, NB * SLOTS], F32)
+        lnb = const.tile([P, NB * SLOTS], F32)
+        for k, dst in enumerate((lnw, lnb)):
+            nc.vector.tensor_copy(
+                out=dst[:].rearrange("p (n u e) -> p u n e", u=2, e=2),
+                in_=lnv[:, 0:2, 2 * NB * k : 2 * NB * k + 2 * NB].rearrange("p u (n e) -> p u n e", e=2),
+            )
+
+        def prep_weights():
+            wgrp = const.tile([P, NB, EMB, SLOTS], BF16, align_bytes=64)
+            nc.vector.tensor_copy(out=wgrp[:], in_=wraw[:].rearrange("p n s e -> p n e s"))
+            wcodes = const.tile([P, NB * EMB], U32, align_bytes=64)
+            wsc = const.tile([P, NB * EMB], U8, align_bytes=64)
+            nc.vector.quantize_mx(
+                out=wcodes[:].bitcast(FP8X4),
+                scales=wsc[:],
+                in_=wgrp[:].rearrange("p n e s -> p (n e s)"),
+            )
+            wq["codes"] = wcodes
+            wq["sc"] = wsc
+
+        def ok(u):
+            return 0 <= u < UNITS
+
+        def in_transposes(u, h):
+            xw = xs[u // GB][:].bitcast(F32)
+            j = u % GB
+            xt = psx.tile([P, SLOTS, P], F32, tag="xt")
+            for s in range(SLOTS):
+                i, r = s // 2, s % 2
+                nc.tensor.transpose(xt[:, s, :], xw[:, r, j, 2 * P * i + P * h : 2 * P * i + P * h + P], ident[:])
+            xts[(u, h)] = xt
+
+        def stats(u, h, q):
+            if q == 0:
+                sts[(u, h)] = small.tile([P, 2, 6], F32, name="st")
+            xb = xts[(u, h)][:].bitcast(BF16)
+            nc.vector.bn_stats(out=sts[(u, h)][:, q, :], in_=xb[:, 2 * q : 2 * q + 2, :])
+
+        def aggregate(u, h):
+            if h == 0:
+                mvs[u] = small.tile([P, 4, 2], F32, name="mv")
+            for e in range(2):
+                nc.vector.bn_aggr(out=mvs[u][:, 2 * h + e, :], in_=sts[(u, h)][:, :, 3 * e : 3 * e + 3])
+
+        def root(u):
+            sd = small.tile([P, 4], F32, name="sd")
+            nc.scalar.activation(out=sd[:], in_=mvs[u][:, :, 1], func=ACT.Sqrt, bias=eps[:, 0:1], scale=1.0)
+            sds[u] = sd
+
+        def inverse(u):
+            rstd = small.tile([P, 4], F32, name="rstd")
+            nc.vector.reciprocal(out=rstd[:], in_=sds[u][:])
+            rstds[u] = rstd
+
+        def shift(u):
+            nmr = small.tile([P, 4], F32, name="nmr")
+            nc.vector.scalar_tensor_tensor(
+                out=nmr[:], in0=mvs[u][:, :, 0], scalar=-1.0, in1=rstds[u][:], op0=ALU.mult, op1=ALU.mult
+            )
+            nmrs[u] = nmr
+
+        def normalise(u, he):
+            if he == 0:
+                ys[u] = work.tile([P, 4, SLOTS, BW], F32, name="y")
+            xv = xts[(u, he // 2)][:].bitcast(BF16).rearrange("p s (k e) -> p s k e", e=2)
+            nc.scalar.activation(
+                out=ys[u][:, he, :, :],
+                in_=xv[:, :, :, he % 2],
+                func=ACT.Identity,
+                scale=rstds[u][:, he : he + 1],
+                bias=nmrs[u][:, he : he + 1],
+            )
+
+        def back_transposes(u, s):
+            yt = psy.tile([P, T], F32, tag="yt")
+            for he in range(4):
+                nc.tensor.transpose(yt[:, P * he : P * he + P], ys[u][:, he, s, :], ident[:])
+            yts[(u, s)] = yt
+
+        def affine(u, s, on_vector=False):
+            if u not in xnps:
+                xnps[u] = work.tile([P, SLOTS, T], BF16, name="xnp")
+            col = SLOTS * (u % NB) + s
+            if on_vector:
+                nc.vector.tensor_scalar(
+                    out=xnps[u][:, s, :],
+                    in0=yts[(u, s)][:],
+                    scalar1=lnw[:, col : col + 1],
+                    scalar2=lnb[:, col : col + 1],
+                    op0=ALU.mult,
+                    op1=ALU.add,
+                )
+            else:
+                nc.scalar.activation(
+                    out=xnps[u][:, s, :],
+                    in_=yts[(u, s)][:],
+                    func=ACT.Identity,
+                    scale=lnw[:, col : col + 1],
+                    bias=lnb[:, col : col + 1],
+                )
+
+        def regroup(u):
+            grp = work.tile([P, T, SLOTS], BF16, align_bytes=64, name="grp")
+            if u >= UNITS - 2:
+                nc.vector.tensor_copy(
+                    out=grp[:].rearrange("p (c i) s -> p c s i", i=4),
+                    in_=xnps[u][:].rearrange("p s (c i) -> p c s i", i=4),
+                )
+            for q in range(4 if u < UNITS - 2 else 0):
+                nc.gpsimd.tensor_scalar(
+                    out=grp[:, P * q : P * q + P, :],
+                    in0=xnps[u][:, :, P * q : P * q + P].rearrange("p s t -> p t s"),
+                    scalar1=1.0,
+                    scalar2=0.0,
+                    op0=ALU.mult,
+                    op1=ALU.add,
+                )
+            grps[u] = grp
+
+        def quantise(u):
+            codes = work.tile([P, T], U32, align_bytes=64, name="codes")
+            sc = work.tile([P, T], U8, align_bytes=64, name="sc")
+            nc.vector.quantize_mx(
+                out=codes[:].bitcast(FP8X4), scales=sc[:], in_=grps[u][:].rearrange("p t s -> p (t s)")
+            )
+            cds[u] = (codes, sc)
+
+        def multiply(u):
+            n = u % NB
+            codes, sc = cds[u]
+            zo = psz.tile([P, 4, EMB], F32, name="zo")
+            for he in range(4):
+                nc.tensor.matmul_mx(
+                    out=zo[:, he, :],
+                    lhsT=codes[:, P * he : P * he + P].bitcast(FP8X4),
+                    lhsT_scale=sc[:, P * he : P * he + P],
+                    rhs=wq["codes"][:, EMB * n : EMB * n + EMB].bitcast(FP8X4),
+                    rhs_scale=wq["sc"][:, EMB * n : EMB * n + EMB],
+                    start=True,
+                    stop=True,
+                )
+            zos[u] = zo
+
+        def finish(u):
+            b, n = u // NB, u % NB
+            zs = work.tile([P, 4, EMB], F32, name="zs")
+            nc.vector.tensor_tensor(
+                out=zs[:],
+                in0=zos[u][:],
+                in1=fcb[:, EMB * n : EMB * n + EMB].unsqueeze(1).to_broadcast([P, 4, EMB]),
+                op=ALU.add,
+            )
+            nc.sync.dma_start(
+                out=out[b, n].rearrange("(h p e) m -> p h (e m)", h=2, e=2),
+                in_=zs[:].rearrange("p (h e) m -> p h (e m)", h=2),
+            )
+
+        for i in range(-3, UNITS + 3):
+            if ok(i - 2):
+                quantise(i - 2)
+            if ok(i - 1):
+                regroup(i - 1)
+            if ok(i) and i % 2 == 0:
+                affine(i, 2, on_vector=True)
+            if ok(i + 1):
+                normalise(i + 1, 0)
+                normalise(i + 1, 1)
+            if ok(i + 3):
+                if (i + 3) % GB == 0 and (i + 3) // GB + 3 < GROUPS:
+                    load((i + 3) // GB + 3, WHOLE)
+                in_transposes(i + 3, 0)
+            if ok(i):
+                affine(i, 0)
+                affine(i, 1)
+                back_transposes(i, 3)
+            if ok(i - 2):
+                multiply(i - 2)
+            if ok(i + 2):
+                root(i + 2)
+            if ok(i + 3):
+                stats(i + 3, 0, 0)
+            if ok(i + 2):
+                inverse(i + 2)
+            if ok(i + 3):
+                stats(i + 3, 0, 1)
+            if ok(i + 2):
+                shift(i + 2)
+            if ok(i + 3):
+                aggregate(i + 3, 0)
+            if ok(i + 1):
+                normalise(i + 1, 2)
+                normalise(i + 1, 3)
+            if ok(i + 3):
+                in_transposes(i + 3, 1)
+            if ok(i - 2):
+                finish(i - 2)
+            if ok(i + 1):
+                back_transposes(i + 1, 0)
+            if ok(i + 3):
+                stats(i + 3, 1, 0)
+                stats(i + 3, 1, 1)
+            if ok(i) and i % 2 == 1:
+                affine(i, 2)
+            if ok(i + 1):
+                back_transposes(i + 1, 1)
+            if ok(i + 3):
+                aggregate(i + 3, 1)
+            if i == -2:
+                prep_weights()
+            if ok(i):
+                affine(i, 3)
+            if ok(i + 1):
+                back_transposes(i + 1, 2)

@@ -17,17 +17,16 @@ SLOTS = 4
 PAIRS = BW // 2
 EPS = 1e-5
 FLOPS = 2 * B * NB * T * (SLOTS * BW) * EMB
-GB = 4
 UNITS = B * NB
-GROUPS = UNITS // GB
-WHOLE = ((0, GB),)
+AHEAD = 8
 
 
 def tile_bandsplitmodule_kernel(tc, x_real, x_imag, ln_w, ln_b, fc_w, fc_b, out):
     nc = tc.nc
     with ExitStack() as ctx:
         const = ctx.enter_context(tc.tile_pool(name="const", bufs=1))
-        xpool = ctx.enter_context(tc.tile_pool(name="xpool", bufs=4))
+        xpool = ctx.enter_context(tc.tile_pool(name="xpool", bufs=AHEAD + 3))
+        zpool = ctx.enter_context(tc.tile_pool(name="zpool", bufs=6))
         work = ctx.enter_context(tc.tile_pool(name="work", bufs=3))
         small = ctx.enter_context(tc.tile_pool(name="small", bufs=8))
         psx = ctx.enter_context(tc.psum_pool(name="psx", bufs=4))
@@ -38,17 +37,16 @@ def tile_bandsplitmodule_kernel(tc, x_real, x_imag, ln_w, ln_b, fc_w, fc_b, out)
         xs, xts, mvs, sds, rstds, nmrs, ys, yts, xnps, grps, zos = {}, {}, {}, {}, {}, {}, {}, {}, {}, {}, {}
         wq, cds, sts = {}, {}, {}
 
-        def load(grp_i, cuts):
-            b, g = grp_i // 2, grp_i % 2
-            xin = xpool.tile([P, 2, GB, 2 * T], BF16, name="xin")
-            for lo, hi in cuts:
-                for r, src in enumerate((x_real, x_imag)):
-                    for c in range(C):
-                        nc.sync.dma_start(
-                            out=xin[PAIRS * c : PAIRS * c + PAIRS, r, lo:hi, :],
-                            in_=src[b, c].rearrange("(n j i) t -> j n (i t)", j=PAIRS, i=2)[:, GB * g + lo : GB * g + hi, :],
-                        )
-            xs[grp_i] = xin
+        def load(u):
+            b, n = u // NB, u % NB
+            xin = xpool.tile([P, 2, 2 * T], BF16, name="xin")
+            for r, src in enumerate((x_real, x_imag)):
+                for c in range(C):
+                    nc.sync.dma_start(
+                        out=xin[PAIRS * c : PAIRS * c + PAIRS, r, :],
+                        in_=src[b, c].rearrange("(n j i) t -> n j (i t)", j=PAIRS, i=2)[n],
+                    )
+            xs[u] = xin
 
         ident = const.tile([P, P], F32)
         make_identity(nc, ident[:])
@@ -61,16 +59,19 @@ def tile_bandsplitmodule_kernel(tc, x_real, x_imag, ln_w, ln_b, fc_w, fc_b, out)
         nc.vector.memset(lnraw[:], 0.0)
         nc.scalar.dma_start(out=lnraw[0:NB, :], in_=ln_w)
         nc.scalar.dma_start(out=lnraw[NB : 2 * NB, :], in_=ln_b)
-        load(0, ((0, 1), (1, GB)))
+        for u in range(3):
+            load(u)
         wraw = const.tile([P, NB, SLOTS, EMB], BF16)
         nc.sync.dma_start(
             out=wraw[:].rearrange("p n s e -> p n (s e)"),
             in_=fc_w.rearrange("n (p s) e -> p n (s e)", s=SLOTS),
         )
-        load(1, WHOLE)
+        for u in range(3, 5):
+            load(u)
         fcb = const.tile([P, NB * EMB], BF16)
         nc.sync.dma_start(out=fcb[:], in_=fc_b.rearrange("n e -> (n e)").partition_broadcast(P))
-        load(2, WHOLE)
+        for u in range(5, AHEAD):
+            load(u)
 
         lnt = psx.tile([P, SLOTS, P], F32, tag="xt")
         lnwords = lnraw[:].bitcast(F32)
@@ -102,12 +103,11 @@ def tile_bandsplitmodule_kernel(tc, x_real, x_imag, ln_w, ln_b, fc_w, fc_b, out)
             return 0 <= u < UNITS
 
         def in_transposes(u, h):
-            xw = xs[u // GB][:].bitcast(F32)
-            j = u % GB
+            xw = xs[u][:].bitcast(F32)
             xt = psx.tile([P, SLOTS, P], F32, tag="xt")
             for s in range(SLOTS):
                 i, r = s // 2, s % 2
-                nc.tensor.transpose(xt[:, s, :], xw[:, r, j, 2 * P * i + P * h : 2 * P * i + P * h + P], ident[:])
+                nc.tensor.transpose(xt[:, s, :], xw[:, r, 2 * P * i + P * h : 2 * P * i + P * h + P], ident[:])
             xts[(u, h)] = xt
 
         def stats(u, h, q):
@@ -223,7 +223,7 @@ def tile_bandsplitmodule_kernel(tc, x_real, x_imag, ln_w, ln_b, fc_w, fc_b, out)
 
         def finish(u):
             b, n = u // NB, u % NB
-            zs = work.tile([P, 4, EMB], F32, name="zs")
+            zs = zpool.tile([P, 4, EMB], F32, name="zs")
             nc.vector.tensor_tensor(
                 out=zs[:],
                 in0=zos[u][:],
@@ -246,8 +246,8 @@ def tile_bandsplitmodule_kernel(tc, x_real, x_imag, ln_w, ln_b, fc_w, fc_b, out)
                 normalise(i + 1, 0)
                 normalise(i + 1, 1)
             if ok(i + 3):
-                if (i + 3) % GB == 0 and (i + 3) // GB + 3 < GROUPS:
-                    load((i + 3) // GB + 3, WHOLE)
+                if ok(i + 3 + AHEAD):
+                    load(i + 3 + AHEAD)
                 in_transposes(i + 3, 0)
             if ok(i):
                 affine(i, 0)

@@ -34,7 +34,7 @@ def tile_bandsplitmodule_kernel(tc, x_real, x_imag, ln_w, ln_b, fc_w, fc_b, out)
         psz = ctx.enter_context(tc.psum_pool(name="psz", bufs=1))
         ctx.enter_context(tc.manual_schedule())
 
-        xs, xts, mvs, sds, rstds, nmrs, ys, yts, xnps, grps, zos = {}, {}, {}, {}, {}, {}, {}, {}, {}, {}, {}
+        xs, xts, mvs, rstds, nmrs, ys, yts, xnps, grps, zos = {}, {}, {}, {}, {}, {}, {}, {}, {}, {}
         wq, cds, sts = {}, {}, {}
 
         def load(u):
@@ -123,20 +123,17 @@ def tile_bandsplitmodule_kernel(tc, x_real, x_imag, ln_w, ln_b, fc_w, fc_b, out)
                 nc.vector.bn_aggr(out=mvs[u][:, 2 * h + e, :], in_=sts[(u, h)][:, :, 3 * e : 3 * e + 3])
 
         def root(u):
-            sd = small.tile([P, 4], F32, name="sd")
-            nc.scalar.activation(out=sd[:], in_=mvs[u][:, :, 1], func=ACT.Sqrt, bias=eps[:, 0:1], scale=1.0)
-            sds[u] = sd
-
-        def inverse(u):
             rstd = small.tile([P, 4], F32, name="rstd")
-            nc.vector.reciprocal(out=rstd[:], in_=sds[u][:])
+            nc.scalar.activation(
+                out=rstd[:], in_=mvs[u][:, :, 1], func=ACT.Abs_reciprocal_sqrt, bias=eps[:, 0:1], scale=1.0
+            )
             rstds[u] = rstd
 
         def shift(u):
+            mr = small.tile([P, 4], F32, name="mr")
+            nc.gpsimd.tensor_tensor(out=mr[:], in0=mvs[u][:, :, 0], in1=rstds[u][:], op=ALU.mult)
             nmr = small.tile([P, 4], F32, name="nmr")
-            nc.vector.scalar_tensor_tensor(
-                out=nmr[:], in0=mvs[u][:, :, 0], scalar=-1.0, in1=rstds[u][:], op0=ALU.mult, op1=ALU.mult
-            )
+            nc.gpsimd.tensor_scalar(out=nmr[:], in0=mr[:], scalar1=-1.0, scalar2=0.0, op0=ALU.mult, op1=ALU.add)
             nmrs[u] = nmr
 
         def normalise(u, he):
@@ -236,11 +233,9 @@ def tile_bandsplitmodule_kernel(tc, x_real, x_imag, ln_w, ln_b, fc_w, fc_b, out)
             )
 
         for i in range(-3, UNITS + 3):
-            if ok(i - 2):
-                quantise(i - 2)
             if ok(i - 1):
                 regroup(i - 1)
-            if ok(i) and i % 2 == 0:
+            if ok(i):
                 affine(i, 2, on_vector=True)
             if ok(i + 1):
                 normalise(i + 1, 0)
@@ -259,12 +254,11 @@ def tile_bandsplitmodule_kernel(tc, x_real, x_imag, ln_w, ln_b, fc_w, fc_b, out)
                 root(i + 2)
             if ok(i + 3):
                 stats(i + 3, 0, 0)
-            if ok(i + 2):
-                inverse(i + 2)
-            if ok(i + 3):
                 stats(i + 3, 0, 1)
             if ok(i + 2):
                 shift(i + 2)
+            if ok(i - 2):
+                finish(i - 2)
             if ok(i + 3):
                 aggregate(i + 3, 0)
             if ok(i + 1):
@@ -272,21 +266,19 @@ def tile_bandsplitmodule_kernel(tc, x_real, x_imag, ln_w, ln_b, fc_w, fc_b, out)
                 normalise(i + 1, 3)
             if ok(i + 3):
                 in_transposes(i + 3, 1)
-            if ok(i - 2):
-                finish(i - 2)
             if ok(i + 1):
                 back_transposes(i + 1, 0)
             if ok(i + 3):
                 stats(i + 3, 1, 0)
                 stats(i + 3, 1, 1)
-            if ok(i) and i % 2 == 1:
-                affine(i, 2)
-            if ok(i + 1):
-                back_transposes(i + 1, 1)
+            if ok(i - 1):
+                quantise(i - 1)
             if ok(i + 3):
                 aggregate(i + 3, 1)
             if i == -2:
                 prep_weights()
+            if ok(i + 1):
+                back_transposes(i + 1, 1)
             if ok(i):
                 affine(i, 3)
             if ok(i + 1):

@@ -183,10 +183,10 @@ def tile_bandsplitmodule_kernel(tc, x_real, x_imag, ln_w, ln_b, fc_w, fc_b, out)
                     out=grp[:].rearrange("p (c i) s -> p c s i", i=4),
                     in_=xnps[u][:].rearrange("p s (c i) -> p c s i", i=4),
                 )
-            for q in range(4 if u < UNITS - 2 else 0):
+            for q in range(2 if u < UNITS - 2 else 0):
                 nc.gpsimd.tensor_scalar(
-                    out=grp[:, P * q : P * q + P, :],
-                    in0=xnps[u][:, :, P * q : P * q + P].rearrange("p s t -> p t s"),
+                    out=grp[:, 2 * P * q : 2 * P * q + 2 * P, :],
+                    in0=xnps[u][:, :, 2 * P * q : 2 * P * q + 2 * P].rearrange("p s t -> p t s"),
                     scalar1=1.0,
                     scalar2=0.0,
                     op0=ALU.mult,

@@ -86,18 +86,28 @@ def tile_bandsplitmodule_kernel(tc, x_real, x_imag, ln_w, ln_b, fc_w, fc_b, out)
                 in_=lnv[:, 0:2, 2 * NB * k : 2 * NB * k + 2 * NB].rearrange("p u (n e) -> p u n e", e=2),
             )
 
-        def prep_weights():
-            wgrp = const.tile([P, NB, EMB, SLOTS], BF16, align_bytes=64)
-            nc.vector.tensor_copy(out=wgrp[:], in_=wraw[:].rearrange("p n s e -> p n e s"))
-            wcodes = const.tile([P, NB * EMB], U32, align_bytes=64)
-            wsc = const.tile([P, NB * EMB], U8, align_bytes=64)
+        wgrp = const.tile([P, NB, EMB, SLOTS], BF16, align_bytes=64)
+        wq["codes"] = const.tile([P, NB * EMB], U32, align_bytes=64, name="wcodes")
+        wq["sc"] = const.tile([P, NB * EMB], U8, align_bytes=64, name="wsc")
+
+        def regroup_weights(k):
+            for n in range(4 * k, 4 * k + 4):
+                nc.gpsimd.tensor_scalar(
+                    out=wgrp[:, n, :, :],
+                    in0=wraw[:, n, :, :].rearrange("p s e -> p e s"),
+                    scalar1=1.0,
+                    scalar2=0.0,
+                    op0=ALU.mult,
+                    op1=ALU.add,
+                )
+
+        def quantise_weights(k):
+            cols = slice(4 * EMB * k, 4 * EMB * k + 4 * EMB)
             nc.vector.quantize_mx(
-                out=wcodes[:].bitcast(FP8X4),
-                scales=wsc[:],
-                in_=wgrp[:].rearrange("p n e s -> p (n e s)"),
+                out=wq["codes"][:, cols].bitcast(FP8X4),
+                scales=wq["sc"][:, cols],
+                in_=wgrp[:, 4 * k : 4 * k + 4, :, :].rearrange("p n e s -> p (n e s)"),
             )
-            wq["codes"] = wcodes
-            wq["sc"] = wsc
 
         def ok(u):
             return 0 <= u < UNITS
@@ -176,14 +186,17 @@ def tile_bandsplitmodule_kernel(tc, x_real, x_imag, ln_w, ln_b, fc_w, fc_b, out)
                     bias=lnb[:, col : col + 1],
                 )
 
-        def regroup(u):
-            grp = work.tile([P, T, SLOTS], BF16, align_bytes=64, name="grp")
+        def regroup(u, q):
+            if q == 0:
+                grps[u] = work.tile([P, T, SLOTS], BF16, align_bytes=64, name="grp")
+            grp = grps[u]
             if u >= UNITS - 2:
-                nc.vector.tensor_copy(
-                    out=grp[:].rearrange("p (c i) s -> p c s i", i=4),
-                    in_=xnps[u][:].rearrange("p s (c i) -> p c s i", i=4),
-                )
-            for q in range(2 if u < UNITS - 2 else 0):
+                if q == 0:
+                    nc.vector.tensor_copy(
+                        out=grp[:].rearrange("p (c i) s -> p c s i", i=4),
+                        in_=xnps[u][:].rearrange("p s (c i) -> p c s i", i=4),
+                    )
+            else:
                 nc.gpsimd.tensor_scalar(
                     out=grp[:, 2 * P * q : 2 * P * q + 2 * P, :],
                     in0=xnps[u][:, :, 2 * P * q : 2 * P * q + 2 * P].rearrange("p s t -> p t s"),
@@ -192,7 +205,6 @@ def tile_bandsplitmodule_kernel(tc, x_real, x_imag, ln_w, ln_b, fc_w, fc_b, out)
                     op0=ALU.mult,
                     op1=ALU.add,
                 )
-            grps[u] = grp
 
         def quantise(u):
             codes = work.tile([P, T], U32, align_bytes=64, name="codes")
@@ -234,7 +246,7 @@ def tile_bandsplitmodule_kernel(tc, x_real, x_imag, ln_w, ln_b, fc_w, fc_b, out)
 
         for i in range(-3, UNITS + 3):
             if ok(i - 1):
-                regroup(i - 1)
+                regroup(i - 1, 0)
             if ok(i):
                 affine(i, 2, on_vector=True)
             if ok(i + 1):
@@ -248,21 +260,21 @@ def tile_bandsplitmodule_kernel(tc, x_real, x_imag, ln_w, ln_b, fc_w, fc_b, out)
                 affine(i, 0)
                 affine(i, 1)
                 back_transposes(i, 3)
-            if ok(i - 2):
-                multiply(i - 2)
-            if ok(i + 2):
-                root(i + 2)
+            if ok(i - 3):
+                multiply(i - 3)
             if ok(i + 3):
                 stats(i + 3, 0, 0)
                 stats(i + 3, 0, 1)
-            if ok(i + 2):
-                shift(i + 2)
-            if ok(i - 2):
-                finish(i - 2)
-            if ok(i + 3):
-                aggregate(i + 3, 0)
             if ok(i + 1):
                 normalise(i + 1, 2)
+            if ok(i + 2):
+                root(i + 2)
+                shift(i + 2)
+            if i in (-1, 0):
+                regroup_weights(i + 1)
+            if ok(i - 1):
+                regroup(i - 1, 1)
+            if ok(i + 1):
                 normalise(i + 1, 3)
             if ok(i + 3):
                 in_transposes(i + 3, 1)
@@ -271,12 +283,15 @@ def tile_bandsplitmodule_kernel(tc, x_real, x_imag, ln_w, ln_b, fc_w, fc_b, out)
             if ok(i + 3):
                 stats(i + 3, 1, 0)
                 stats(i + 3, 1, 1)
-            if ok(i - 1):
-                quantise(i - 1)
+                aggregate(i + 3, 0)
+            if ok(i - 3):
+                finish(i - 3)
             if ok(i + 3):
                 aggregate(i + 3, 1)
-            if i == -2:
-                prep_weights()
+            if i in (0, 1):
+                quantise_weights(i)
+            if ok(i - 2):
+                quantise(i - 2)
             if ok(i + 1):
                 back_transposes(i + 1, 1)
             if ok(i):

@@ -18,7 +18,9 @@ PAIRS = BW // 2
 EPS = 1e-5
 FLOPS = 2 * B * NB * T * (SLOTS * BW) * EMB
 UNITS = B * NB
+WEIGHT_ROUNDS = {-2: (0, 2), -1: (2, 6), 0: (6, 8)}
 AHEAD = 8
+SHARE = 384
 
 
 def tile_bandsplitmodule_kernel(tc, x_real, x_imag, ln_w, ln_b, fc_w, fc_b, out):
@@ -37,15 +39,17 @@ def tile_bandsplitmodule_kernel(tc, x_real, x_imag, ln_w, ln_b, fc_w, fc_b, out)
         xs, xts, mvs, rstds, nmrs, ys, yts, xnps, grps, zos = {}, {}, {}, {}, {}, {}, {}, {}, {}, {}
         wq, cds, sts = {}, {}, {}
 
-        def load(u):
+        def load(u, parts=1):
             b, n = u // NB, u % NB
-            xin = xpool.tile([P, 2, 2 * T], BF16, name="xin")
-            for r, src in enumerate((x_real, x_imag)):
-                for c in range(C):
-                    nc.sync.dma_start(
-                        out=xin[PAIRS * c : PAIRS * c + PAIRS, r, :],
-                        in_=src[b, c].rearrange("(n j i) t -> n j (i t)", j=PAIRS, i=2)[n],
-                    )
+            xin = xpool.tile([P, 2, 2, T], BF16, name="xin")
+            for h in range(parts):
+                ts = slice(T // parts * h, T // parts * (h + 1))
+                for r, src in enumerate((x_real, x_imag)):
+                    for c in range(C):
+                        nc.sync.dma_start(
+                            out=xin[PAIRS * c : PAIRS * c + PAIRS, r, :, ts],
+                            in_=src[b, c].rearrange("(n j i) t -> n j i t", j=PAIRS, i=2)[n][:, :, ts],
+                        )
             xs[u] = xin
 
         ident = const.tile([P, P], F32)
@@ -59,39 +63,41 @@ def tile_bandsplitmodule_kernel(tc, x_real, x_imag, ln_w, ln_b, fc_w, fc_b, out)
         nc.vector.memset(lnraw[:], 0.0)
         nc.scalar.dma_start(out=lnraw[0:NB, :], in_=ln_w)
         nc.scalar.dma_start(out=lnraw[NB : 2 * NB, :], in_=ln_b)
-        for u in range(3):
-            load(u)
+        load(0, parts=2)
+        load(1)
         wraw = const.tile([P, NB, SLOTS, EMB], BF16)
         nc.sync.dma_start(
             out=wraw[:].rearrange("p n s e -> p n (s e)"),
             in_=fc_w.rearrange("n (p s) e -> p n (s e)", s=SLOTS),
         )
-        for u in range(3, 5):
+        for u in range(2, 5):
             load(u)
         fcb = const.tile([P, NB * EMB], BF16)
         nc.sync.dma_start(out=fcb[:], in_=fc_b.rearrange("n e -> (n e)").partition_broadcast(P))
         for u in range(5, AHEAD):
             load(u)
 
-        lnt = psx.tile([P, SLOTS, P], F32, tag="xt")
         lnwords = lnraw[:].bitcast(F32)
-        for u in range(2):
-            nc.tensor.transpose(lnt[:, u, :], lnwords[:, u::2], ident[:])
-        lnv = lnt[:].bitcast(BF16)
         lnw = const.tile([P, NB * SLOTS], F32)
         lnb = const.tile([P, NB * SLOTS], F32)
-        for k, dst in enumerate((lnw, lnb)):
-            nc.vector.tensor_copy(
-                out=dst[:].rearrange("p (n u e) -> p u n e", u=2, e=2),
-                in_=lnv[:, 0:2, 2 * NB * k : 2 * NB * k + 2 * NB].rearrange("p u (n e) -> p u n e", e=2),
-            )
+
+        def gains():
+            lnt = psy.tile([P, T], F32, tag="yt")
+            for u in range(2):
+                nc.tensor.transpose(lnt[:, P * u : P * u + P], lnwords[:, u::2], ident[:])
+            lnv = lnt[:].bitcast(BF16).rearrange("p (u q) -> p u q", u=4)
+            for k, dst in enumerate((lnw, lnb)):
+                nc.vector.tensor_copy(
+                    out=dst[:].rearrange("p (n u e) -> p u n e", u=2, e=2),
+                    in_=lnv[:, 0:2, 2 * NB * k : 2 * NB * k + 2 * NB].rearrange("p u (n e) -> p u n e", e=2),
+                )
 
         wgrp = const.tile([P, NB, EMB, SLOTS], BF16, align_bytes=64)
         wq["codes"] = const.tile([P, NB * EMB], U32, align_bytes=64, name="wcodes")
         wq["sc"] = const.tile([P, NB * EMB], U8, align_bytes=64, name="wsc")
 
-        def regroup_weights(k):
-            for n in range(4 * k, 4 * k + 4):
+        def regroup_weights(lo, hi):
+            for n in range(lo, hi):
                 nc.gpsimd.tensor_scalar(
                     out=wgrp[:, n, :, :],
                     in0=wraw[:, n, :, :].rearrange("p s e -> p e s"),
@@ -113,7 +119,7 @@ def tile_bandsplitmodule_kernel(tc, x_real, x_imag, ln_w, ln_b, fc_w, fc_b, out)
             return 0 <= u < UNITS
 
         def in_transposes(u, h):
-            xw = xs[u][:].bitcast(F32)
+            xw = xs[u][:].rearrange("p r i t -> p r (i t)").bitcast(F32)
             xt = psx.tile([P, SLOTS, P], F32, tag="xt")
             for s in range(SLOTS):
                 i, r = s // 2, s % 2
@@ -132,19 +138,27 @@ def tile_bandsplitmodule_kernel(tc, x_real, x_imag, ln_w, ln_b, fc_w, fc_b, out)
             for e in range(2):
                 nc.vector.bn_aggr(out=mvs[u][:, 2 * h + e, :], in_=sts[(u, h)][:, :, 3 * e : 3 * e + 3])
 
-        def root(u):
-            rstd = small.tile([P, 4], F32, name="rstd")
+        def root(u, lo=0, hi=4):
+            if lo == 0:
+                rstds[u] = small.tile([P, 4], F32, name="rstd")
             nc.scalar.activation(
-                out=rstd[:], in_=mvs[u][:, :, 1], func=ACT.Abs_reciprocal_sqrt, bias=eps[:, 0:1], scale=1.0
+                out=rstds[u][:, lo:hi],
+                in_=mvs[u][:, lo:hi, 1],
+                func=ACT.Abs_reciprocal_sqrt,
+                bias=eps[:, 0:1],
+                scale=1.0,
             )
-            rstds[u] = rstd
 
-        def shift(u):
+        def shift(u, lo=0, hi=4):
+            if lo == 0:
+                nmrs[u] = small.tile([P, 4], F32, name="nmr")
             mr = small.tile([P, 4], F32, name="mr")
-            nc.gpsimd.tensor_tensor(out=mr[:], in0=mvs[u][:, :, 0], in1=rstds[u][:], op=ALU.mult)
-            nmr = small.tile([P, 4], F32, name="nmr")
-            nc.gpsimd.tensor_scalar(out=nmr[:], in0=mr[:], scalar1=-1.0, scalar2=0.0, op0=ALU.mult, op1=ALU.add)
-            nmrs[u] = nmr
+            nc.gpsimd.tensor_tensor(
+                out=mr[:, lo:hi], in0=mvs[u][:, lo:hi, 0], in1=rstds[u][:, lo:hi], op=ALU.mult
+            )
+            nc.gpsimd.tensor_scalar(
+                out=nmrs[u][:, lo:hi], in0=mr[:, lo:hi], scalar1=-1.0, scalar2=0.0, op0=ALU.mult, op1=ALU.add
+            )
 
         def normalise(u, he):
             if he == 0:
@@ -164,14 +178,14 @@ def tile_bandsplitmodule_kernel(tc, x_real, x_imag, ln_w, ln_b, fc_w, fc_b, out)
                 nc.tensor.transpose(yt[:, P * he : P * he + P], ys[u][:, he, s, :], ident[:])
             yts[(u, s)] = yt
 
-        def affine(u, s, on_vector=False):
+        def affine(u, s, lo=0, hi=T, on_vector=False):
             if u not in xnps:
                 xnps[u] = work.tile([P, SLOTS, T], BF16, name="xnp")
             col = SLOTS * (u % NB) + s
             if on_vector:
                 nc.vector.tensor_scalar(
-                    out=xnps[u][:, s, :],
-                    in0=yts[(u, s)][:],
+                    out=xnps[u][:, s, lo:hi],
+                    in0=yts[(u, s)][:, lo:hi],
                     scalar1=lnw[:, col : col + 1],
                     scalar2=lnb[:, col : col + 1],
                     op0=ALU.mult,
@@ -179,8 +193,8 @@ def tile_bandsplitmodule_kernel(tc, x_real, x_imag, ln_w, ln_b, fc_w, fc_b, out)
                 )
             else:
                 nc.scalar.activation(
-                    out=xnps[u][:, s, :],
-                    in_=yts[(u, s)][:],
+                    out=xnps[u][:, s, lo:hi],
+                    in_=yts[(u, s)][:, lo:hi],
                     func=ACT.Identity,
                     scale=lnw[:, col : col + 1],
                     bias=lnb[:, col : col + 1],
@@ -189,22 +203,21 @@ def tile_bandsplitmodule_kernel(tc, x_real, x_imag, ln_w, ln_b, fc_w, fc_b, out)
         def regroup(u, q):
             if q == 0:
                 grps[u] = work.tile([P, T, SLOTS], BF16, align_bytes=64, name="grp")
-            grp = grps[u]
-            if u >= UNITS - 2:
-                if q == 0:
-                    nc.vector.tensor_copy(
-                        out=grp[:].rearrange("p (c i) s -> p c s i", i=4),
-                        in_=xnps[u][:].rearrange("p s (c i) -> p c s i", i=4),
-                    )
-            else:
-                nc.gpsimd.tensor_scalar(
-                    out=grp[:, 2 * P * q : 2 * P * q + 2 * P, :],
-                    in0=xnps[u][:, :, 2 * P * q : 2 * P * q + 2 * P].rearrange("p s t -> p t s"),
-                    scalar1=1.0,
-                    scalar2=0.0,
-                    op0=ALU.mult,
-                    op1=ALU.add,
-                )
+            nc.gpsimd.tensor_scalar(
+                out=grps[u][:, 2 * P * q : 2 * P * q + 2 * P, :],
+                in0=xnps[u][:, :, 2 * P * q : 2 * P * q + 2 * P].rearrange("p s t -> p t s"),
+                scalar1=1.0,
+                scalar2=0.0,
+                op0=ALU.mult,
+                op1=ALU.add,
+            )
+
+        def regroup_on_vector(u):
+            grps[u] = work.tile([P, T, SLOTS], BF16, align_bytes=64, name="grp")
+            nc.vector.tensor_copy(
+                out=grps[u][:].rearrange("p (c i) s -> p c s i", i=4),
+                in_=xnps[u][:].rearrange("p s (c i) -> p c s i", i=4),
+            )
 
         def quantise(u):
             codes = work.tile([P, T], U32, align_bytes=64, name="codes")
@@ -244,12 +257,24 @@ def tile_bandsplitmodule_kernel(tc, x_real, x_imag, ln_w, ln_b, fc_w, fc_b, out)
                 in_=zs[:].rearrange("p (h e) m -> p h (e m)", h=2),
             )
 
-        for i in range(-3, UNITS + 3):
+        for h in range(2):
+            in_transposes(0, h)
+            stats(0, h, 0)
+            stats(0, h, 1)
+            aggregate(0, h)
+            root(0, 2 * h, 2 * h + 2)
+            shift(0, 2 * h, 2 * h + 2)
+            normalise(0, 2 * h)
+            normalise(0, 2 * h + 1)
+        load(AHEAD)
+        gains()
+
+        for i in range(-2, UNITS - 2):
             if ok(i - 1):
                 regroup(i - 1, 0)
             if ok(i):
-                affine(i, 2, on_vector=True)
-            if ok(i + 1):
+                affine(i, 2, 0, SHARE, on_vector=True)
+            if i >= 0:
                 normalise(i + 1, 0)
                 normalise(i + 1, 1)
             if ok(i + 3):
@@ -265,16 +290,16 @@ def tile_bandsplitmodule_kernel(tc, x_real, x_imag, ln_w, ln_b, fc_w, fc_b, out)
             if ok(i + 3):
                 stats(i + 3, 0, 0)
                 stats(i + 3, 0, 1)
-            if ok(i + 1):
+            if i >= 0:
                 normalise(i + 1, 2)
-            if ok(i + 2):
+            if i >= -1:
                 root(i + 2)
                 shift(i + 2)
-            if i in (-1, 0):
-                regroup_weights(i + 1)
+            if i in WEIGHT_ROUNDS:
+                regroup_weights(*WEIGHT_ROUNDS[i])
             if ok(i - 1):
                 regroup(i - 1, 1)
-            if ok(i + 1):
+            if i >= 0:
                 normalise(i + 1, 3)
             if ok(i + 3):
                 in_transposes(i + 3, 1)
@@ -296,5 +321,43 @@ def tile_bandsplitmodule_kernel(tc, x_real, x_imag, ln_w, ln_b, fc_w, fc_b, out)
                 back_transposes(i + 1, 1)
             if ok(i):
                 affine(i, 3)
+                affine(i, 2, SHARE, T)
             if ok(i + 1):
                 back_transposes(i + 1, 2)
+
+        a, z = UNITS - 2, UNITS - 1
+        regroup(a - 1, 0)
+        regroup(a - 1, 1)
+        normalise(z, 0)
+        normalise(z, 1)
+        affine(a, 0)
+        affine(a, 1)
+        back_transposes(a, 3)
+        multiply(a - 3)
+        normalise(z, 2)
+        normalise(z, 3)
+        back_transposes(z, 0)
+        back_transposes(z, 1)
+        finish(a - 3)
+        quantise(a - 2)
+        affine(a, 2)
+        affine(a, 3)
+        back_transposes(z, 2)
+        multiply(a - 2)
+        regroup_on_vector(a)
+        quantise(a - 1)
+        affine(z, 0)
+        affine(z, 1)
+        back_transposes(z, 3)
+        finish(a - 2)
+        multiply(a - 1)
+        quantise(a)
+        affine(z, 2)
+        affine(z, 3)
+        finish(a - 1)
+        multiply(a)
+        regroup_on_vector(z)
+        finish(a)
+        quantise(z)
+        multiply(z)
+        finish(z)

@@ -118,9 +118,22 @@ def tile_bandsplitmodule_kernel(tc, x_real, x_imag, ln_w, ln_b, fc_w, fc_b, out)
         def ok(u):
             return 0 <= u < UNITS
 
-        def in_transposes(u, h):
+        def keep_busy(bank, passes):
+            for k in range(passes):
+                nc.tensor.matmul_mx(
+                    out=bank,
+                    lhsT=wq["codes"][:, 0:EMB].bitcast(FP8X4),
+                    lhsT_scale=wq["sc"][:, 0:EMB],
+                    rhs=wq["codes"][:, 0:T].bitcast(FP8X4),
+                    rhs_scale=wq["sc"][:, 0:T],
+                    start=True,
+                    stop=True,
+                )
+
+        def in_transposes(u, h, busy=0):
             xw = xs[u][:].rearrange("p r i t -> p r (i t)").bitcast(F32)
             xt = psx.tile([P, SLOTS, P], F32, tag="xt")
+            keep_busy(xt[:].rearrange("p s t -> p (s t)"), busy)
             for s in range(SLOTS):
                 i, r = s // 2, s % 2
                 nc.tensor.transpose(xt[:, s, :], xw[:, r, 2 * P * i + P * h : 2 * P * i + P * h + P], ident[:])
@@ -227,10 +240,11 @@ def tile_bandsplitmodule_kernel(tc, x_real, x_imag, ln_w, ln_b, fc_w, fc_b, out)
             )
             cds[u] = (codes, sc)
 
-        def multiply(u):
+        def multiply(u, busy=0):
             n = u % NB
             codes, sc = cds[u]
             zo = psz.tile([P, 4, EMB], F32, name="zo")
+            keep_busy(zo[:].rearrange("p h e -> p (h e)"), busy)
             for he in range(4):
                 nc.tensor.matmul_mx(
                     out=zo[:, he, :],
@@ -280,13 +294,13 @@ def tile_bandsplitmodule_kernel(tc, x_real, x_imag, ln_w, ln_b, fc_w, fc_b, out)
             if ok(i + 3):
                 if ok(i + 3 + AHEAD):
                     load(i + 3 + AHEAD)
-                in_transposes(i + 3, 0)
+                in_transposes(i + 3, 0, busy=2 if i >= 2 else 0)
             if ok(i):
                 affine(i, 0)
                 affine(i, 1)
                 back_transposes(i, 3)
             if ok(i - 3):
-                multiply(i - 3)
+                multiply(i - 3, busy=1)
             if ok(i + 3):
                 stats(i + 3, 0, 0)
                 stats(i + 3, 0, 1)

@@ -39,14 +39,14 @@ def tile_bandsplitmodule_kernel(tc, x_real, x_imag, ln_w, ln_b, fc_w, fc_b, out)
         xs, xts, mvs, rstds, nmrs, ys, yts, xnps, grps, zos = {}, {}, {}, {}, {}, {}, {}, {}, {}, {}
         wq, cds, sts = {}, {}, {}
 
-        def load(u, parts=1):
+        def load(u, parts=1, queues=(nc.sync, nc.sync)):
             b, n = u // NB, u % NB
             xin = xpool.tile([P, 2, 2, T], BF16, name="xin")
             for h in range(parts):
                 ts = slice(T // parts * h, T // parts * (h + 1))
                 for r, src in enumerate((x_real, x_imag)):
                     for c in range(C):
-                        nc.sync.dma_start(
+                        queues[c].dma_start(
                             out=xin[PAIRS * c : PAIRS * c + PAIRS, r, :, ts],
                             in_=src[b, c].rearrange("(n j i) t -> n j i t", j=PAIRS, i=2)[n][:, :, ts],
                         )
@@ -61,9 +61,9 @@ def tile_bandsplitmodule_kernel(tc, x_real, x_imag, ln_w, ln_b, fc_w, fc_b, out)
 
         lnraw = const.tile([P, SLOTS * BW], BF16)
         nc.vector.memset(lnraw[:], 0.0)
+        load(0, parts=2, queues=(nc.sync, nc.scalar))
         nc.scalar.dma_start(out=lnraw[0:NB, :], in_=ln_w)
         nc.scalar.dma_start(out=lnraw[NB : 2 * NB, :], in_=ln_b)
-        load(0, parts=2)
         load(1)
         wraw = const.tile([P, NB, SLOTS, EMB], BF16)
         nc.sync.dma_start(
@@ -114,6 +114,12 @@ def tile_bandsplitmodule_kernel(tc, x_real, x_imag, ln_w, ln_b, fc_w, fc_b, out)
                 scales=wq["sc"][:, cols],
                 in_=wgrp[:, 4 * k : 4 * k + 4, :, :].rearrange("p n e s -> p (n e s)"),
             )
+
+        def frames(h):
+            return slice(0, T) if h is None else slice(T // 2 * h, T // 2 * h + T // 2)
+
+        def blocks(h):
+            return list(range(4)) if h is None else [2 * h, 2 * h + 1]
 
         def ok(u):
             return 0 <= u < UNITS
@@ -225,29 +231,39 @@ def tile_bandsplitmodule_kernel(tc, x_real, x_imag, ln_w, ln_b, fc_w, fc_b, out)
                 op1=ALU.add,
             )
 
-        def regroup_on_vector(u):
-            grps[u] = work.tile([P, T, SLOTS], BF16, align_bytes=64, name="grp")
+        def regroup_on_vector(u, h=None):
+            fs = frames(h)
+            if fs.start == 0:
+                grps[u] = work.tile([P, T, SLOTS], BF16, align_bytes=64, name="grp")
             nc.vector.tensor_copy(
-                out=grps[u][:].rearrange("p (c i) s -> p c s i", i=4),
-                in_=xnps[u][:].rearrange("p s (c i) -> p c s i", i=4),
+                out=grps[u][:, fs, :].rearrange("p (c i) s -> p c s i", i=4),
+                in_=xnps[u][:, :, fs].rearrange("p s (c i) -> p c s i", i=4),
             )
 
-        def quantise(u):
-            codes = work.tile([P, T], U32, align_bytes=64, name="codes")
-            sc = work.tile([P, T], U8, align_bytes=64, name="sc")
+        def quantise(u, h=None):
+            fs = frames(h)
+            if fs.start == 0:
+                codes = work.tile([P, T], U32, align_bytes=64, name="codes")
+                sc = work.tile([P, T], U8, align_bytes=64, name="sc")
+                cds[u] = (codes, sc)
+            codes, sc = cds[u]
             nc.vector.quantize_mx(
-                out=codes[:].bitcast(FP8X4), scales=sc[:], in_=grps[u][:].rearrange("p t s -> p (t s)")
+                out=codes[:, fs].bitcast(FP8X4),
+                scales=sc[:, fs],
+                in_=grps[u][:, fs, :].rearrange("p t s -> p (t s)"),
             )
-            cds[u] = (codes, sc)
 
-        def multiply(u, busy=0):
+        def multiply(u, h=None, busy=0):
             n = u % NB
             codes, sc = cds[u]
-            zo = psz.tile([P, 4, EMB], F32, name="zo")
-            keep_busy(zo[:].rearrange("p h e -> p (h e)"), busy)
-            for he in range(4):
+            if h is None:
+                zo = psz.tile([P, 4 * EMB], F32, name="zo")
+            else:
+                zo = psy.tile([P, T], F32, tag="yt")
+            keep_busy(zo[:], busy)
+            for k, he in enumerate(blocks(h)):
                 nc.tensor.matmul_mx(
-                    out=zo[:, he, :],
+                    out=zo[:, EMB * k : EMB * k + EMB],
                     lhsT=codes[:, P * he : P * he + P].bitcast(FP8X4),
                     lhsT_scale=sc[:, P * he : P * he + P],
                     rhs=wq["codes"][:, EMB * n : EMB * n + EMB].bitcast(FP8X4),
@@ -255,20 +271,21 @@ def tile_bandsplitmodule_kernel(tc, x_real, x_imag, ln_w, ln_b, fc_w, fc_b, out)
                     start=True,
                     stop=True,
                 )
-            zos[u] = zo
+            zos[(u, h)] = zo
 
-        def finish(u):
+        def finish(u, h=None):
             b, n = u // NB, u % NB
+            hes = blocks(h)
             zs = zpool.tile([P, 4, EMB], F32, name="zs")
             nc.vector.tensor_tensor(
-                out=zs[:],
-                in0=zos[u][:],
-                in1=fcb[:, EMB * n : EMB * n + EMB].unsqueeze(1).to_broadcast([P, 4, EMB]),
+                out=zs[:, 0 : len(hes), :],
+                in0=zos[(u, h)][:, 0 : len(hes) * EMB].rearrange("p (k m) -> p k m", m=EMB),
+                in1=fcb[:, EMB * n : EMB * n + EMB].unsqueeze(1).to_broadcast([P, len(hes), EMB]),
                 op=ALU.add,
             )
             nc.sync.dma_start(
-                out=out[b, n].rearrange("(h p e) m -> p h (e m)", h=2, e=2),
-                in_=zs[:].rearrange("p (h e) m -> p h (e m)", h=2),
+                out=out[b, n].rearrange("(h p e) m -> p h (e m)", h=2, e=2)[:, hes[0] // 2 : hes[-1] // 2 + 1, :],
+                in_=zs[:, 0 : len(hes), :].rearrange("p (h e) m -> p h (e m)", e=2),
             )
 
         for h in range(2):
@@ -340,38 +357,42 @@ def tile_bandsplitmodule_kernel(tc, x_real, x_imag, ln_w, ln_b, fc_w, fc_b, out)
                 back_transposes(i + 1, 2)
 
         a, z = UNITS - 2, UNITS - 1
-        regroup(a - 1, 0)
-        regroup(a - 1, 1)
+        quantise(a - 2)
         normalise(z, 0)
         normalise(z, 1)
         affine(a, 0)
         affine(a, 1)
         back_transposes(a, 3)
         multiply(a - 3)
+        regroup_on_vector(a - 1)
         normalise(z, 2)
         normalise(z, 3)
         back_transposes(z, 0)
         back_transposes(z, 1)
         finish(a - 3)
-        quantise(a - 2)
+        multiply(a - 2)
+        quantise(a - 1)
         affine(a, 2)
         affine(a, 3)
         back_transposes(z, 2)
-        multiply(a - 2)
+        finish(a - 2)
+        multiply(a - 1)
         regroup_on_vector(a)
-        quantise(a - 1)
         affine(z, 0)
         affine(z, 1)
         back_transposes(z, 3)
-        finish(a - 2)
-        multiply(a - 1)
-        quantise(a)
-        affine(z, 2)
-        affine(z, 3)
         finish(a - 1)
+        quantise(a)
+        for lo, hi in ((0, T // 2), (T // 2, T)):
+            affine(z, 2, lo, hi)
+            affine(z, 3, lo, hi)
         multiply(a)
-        regroup_on_vector(z)
+        regroup_on_vector(z, 0)
+        regroup_on_vector(z, 1)
+        quantise(z, 0)
+        multiply(z, 0)
+        quantise(z, 1)
+        multiply(z, 1)
         finish(a)
-        quantise(z)
-        multiply(z)
-        finish(z)
+        finish(z, 0)
+        finish(z, 1)

from contextlib import ExitStack

import concourse.mybir as mybir
from concourse.masks import make_identity

F32 = mybir.dt.float32
BF16 = mybir.dt.bfloat16
U32 = mybir.dt.uint32
U8 = mybir.dt.uint8
FP8X4 = mybir.dt.float8_e4m3fn_x4
ACT = mybir.ActivationFunctionType
ALU = mybir.AluOpType

B, C, NB, BW, T, EMB = 4, 2, 8, 128, 512, 128
P = 128
SLOTS = 4
PAIRS = BW // 2
EPS = 1e-5
FLOPS = 2 * B * NB * T * (SLOTS * BW) * EMB
UNITS = B * NB
WEIGHT_ROUNDS = {-2: (0, 2), -1: (2, 6), 0: (6, 8)}
AHEAD = 8
SHARE = 384


def tile_bandsplitmodule_kernel(tc, x_real, x_imag, ln_w, ln_b, fc_w, fc_b, out):
    nc = tc.nc
    with ExitStack() as ctx:
        const = ctx.enter_context(tc.tile_pool(name="const", bufs=1))
        xpool = ctx.enter_context(tc.tile_pool(name="xpool", bufs=AHEAD + 3))
        zpool = ctx.enter_context(tc.tile_pool(name="zpool", bufs=6))
        work = ctx.enter_context(tc.tile_pool(name="work", bufs=3))
        small = ctx.enter_context(tc.tile_pool(name="small", bufs=8))
        psx = ctx.enter_context(tc.psum_pool(name="psx", bufs=4))
        psy = ctx.enter_context(tc.psum_pool(name="psy", bufs=3))
        psz = ctx.enter_context(tc.psum_pool(name="psz", bufs=1))
        ctx.enter_context(tc.manual_schedule())

        xs, xts, mvs, rstds, nmrs, ys, yts, xnps, grps, zos = {}, {}, {}, {}, {}, {}, {}, {}, {}, {}
        wq, cds, sts = {}, {}, {}

        def load(u, parts=1, queues=(nc.sync, nc.sync)):
            b, n = u // NB, u % NB
            xin = xpool.tile([P, 2, 2, T], BF16, name="xin")
            for h in range(parts):
                ts = slice(T // parts * h, T // parts * (h + 1))
                for r, src in enumerate((x_real, x_imag)):
                    for c in range(C):
                        queues[c].dma_start(
                            out=xin[PAIRS * c : PAIRS * c + PAIRS, r, :, ts],
                            in_=src[b, c].rearrange("(n j i) t -> n j i t", j=PAIRS, i=2)[n][:, :, ts],
                        )
            xs[u] = xin

        ident = const.tile([P, P], F32)
        make_identity(nc, ident[:])
        zero1 = const.tile([P, 1], F32)
        nc.vector.memset(zero1[:], 0.0)
        eps = const.tile([P, 1], F32)
        nc.vector.tensor_scalar(out=eps[:], in0=zero1[:], scalar1=EPS, scalar2=None, op0=ALU.add)

        lnraw = const.tile([P, SLOTS * BW], BF16)
        nc.vector.memset(lnraw[:], 0.0)
        load(0, parts=2, queues=(nc.sync, nc.scalar))
        nc.scalar.dma_start(out=lnraw[0:NB, :], in_=ln_w)
        nc.scalar.dma_start(out=lnraw[NB : 2 * NB, :], in_=ln_b)
        load(1)
        wraw = const.tile([P, NB, SLOTS, EMB], BF16)
        nc.sync.dma_start(
            out=wraw[:].rearrange("p n s e -> p n (s e)"),
            in_=fc_w.rearrange("n (p s) e -> p n (s e)", s=SLOTS),
        )
        for u in range(2, 5):
            load(u)
        fcb = const.tile([P, NB * EMB], BF16)
        nc.sync.dma_start(out=fcb[:], in_=fc_b.rearrange("n e -> (n e)").partition_broadcast(P))
        for u in range(5, AHEAD):
            load(u)

        lnwords = lnraw[:].bitcast(F32)
        lnw = const.tile([P, NB * SLOTS], F32)
        lnb = const.tile([P, NB * SLOTS], F32)

        def gains():
            lnt = psy.tile([P, T], F32, tag="yt")
            for u in range(2):
                nc.tensor.transpose(lnt[:, P * u : P * u + P], lnwords[:, u::2], ident[:])
            lnv = lnt[:].bitcast(BF16).rearrange("p (u q) -> p u q", u=4)
            for k, dst in enumerate((lnw, lnb)):
                nc.vector.tensor_copy(
                    out=dst[:].rearrange("p (n u e) -> p u n e", u=2, e=2),
                    in_=lnv[:, 0:2, 2 * NB * k : 2 * NB * k + 2 * NB].rearrange("p u (n e) -> p u n e", e=2),
                )

        wgrp = const.tile([P, NB, EMB, SLOTS], BF16, align_bytes=64)
        wq["codes"] = const.tile([P, NB * EMB], U32, align_bytes=64, name="wcodes")
        wq["sc"] = const.tile([P, NB * EMB], U8, align_bytes=64, name="wsc")

        def regroup_weights(lo, hi):
            for n in range(lo, hi):
                nc.gpsimd.tensor_scalar(
                    out=wgrp[:, n, :, :],
                    in0=wraw[:, n, :, :].rearrange("p s e -> p e s"),
                    scalar1=1.0,
                    scalar2=0.0,
                    op0=ALU.mult,
                    op1=ALU.add,
                )

        def quantise_weights(k):
            cols = slice(4 * EMB * k, 4 * EMB * k + 4 * EMB)
            nc.vector.quantize_mx(
                out=wq["codes"][:, cols].bitcast(FP8X4),
                scales=wq["sc"][:, cols],
                in_=wgrp[:, 4 * k : 4 * k + 4, :, :].rearrange("p n e s -> p (n e s)"),
            )

        def frames(h):
            return slice(0, T) if h is None else slice(T // 2 * h, T // 2 * h + T // 2)

        def blocks(h):
            return list(range(4)) if h is None else [2 * h, 2 * h + 1]

        def ok(u):
            return 0 <= u < UNITS

        def keep_busy(bank, passes):
            for k in range(passes):
                nc.tensor.matmul_mx(
                    out=bank,
                    lhsT=wq["codes"][:, 0:EMB].bitcast(FP8X4),
                    lhsT_scale=wq["sc"][:, 0:EMB],
                    rhs=wq["codes"][:, 0:T].bitcast(FP8X4),
                    rhs_scale=wq["sc"][:, 0:T],
                    start=True,
                    stop=True,
                )

        def in_transposes(u, h, busy=0):
            xw = xs[u][:].rearrange("p r i t -> p r (i t)").bitcast(F32)
            xt = psx.tile([P, SLOTS, P], F32, tag="xt")
            keep_busy(xt[:].rearrange("p s t -> p (s t)"), busy)
            for s in range(SLOTS):
                i, r = s // 2, s % 2
                nc.tensor.transpose(xt[:, s, :], xw[:, r, 2 * P * i + P * h : 2 * P * i + P * h + P], ident[:])
            xts[(u, h)] = xt

        def stats(u, h, q):
            if q == 0:
                sts[(u, h)] = small.tile([P, 2, 6], F32, name="st")
            xb = xts[(u, h)][:].bitcast(BF16)
            nc.vector.bn_stats(out=sts[(u, h)][:, q, :], in_=xb[:, 2 * q : 2 * q + 2, :])

        def aggregate(u, h):
            if h == 0:
                mvs[u] = small.tile([P, 4, 2], F32, name="mv")
            for e in range(2):
                nc.vector.bn_aggr(out=mvs[u][:, 2 * h + e, :], in_=sts[(u, h)][:, :, 3 * e : 3 * e + 3])

        def root(u, lo=0, hi=4):
            if lo == 0:
                rstds[u] = small.tile([P, 4], F32, name="rstd")
            nc.scalar.activation(
                out=rstds[u][:, lo:hi],
                in_=mvs[u][:, lo:hi, 1],
                func=ACT.Abs_reciprocal_sqrt,
                bias=eps[:, 0:1],
                scale=1.0,
            )

        def shift(u, lo=0, hi=4):
            if lo == 0:
                nmrs[u] = small.tile([P, 4], F32, name="nmr")
            mr = small.tile([P, 4], F32, name="mr")
            nc.gpsimd.tensor_tensor(
                out=mr[:, lo:hi], in0=mvs[u][:, lo:hi, 0], in1=rstds[u][:, lo:hi], op=ALU.mult
            )
            nc.gpsimd.tensor_scalar(
                out=nmrs[u][:, lo:hi], in0=mr[:, lo:hi], scalar1=-1.0, scalar2=0.0, op0=ALU.mult, op1=ALU.add
            )

        def normalise(u, he):
            if he == 0:
                ys[u] = work.tile([P, 4, SLOTS, BW], F32, name="y")
            xv = xts[(u, he // 2)][:].bitcast(BF16).rearrange("p s (k e) -> p s k e", e=2)
            nc.scalar.activation(
                out=ys[u][:, he, :, :],
                in_=xv[:, :, :, he % 2],
                func=ACT.Identity,
                scale=rstds[u][:, he : he + 1],
                bias=nmrs[u][:, he : he + 1],
            )

        def back_transposes(u, s):
            yt = psy.tile([P, T], F32, tag="yt")
            for he in range(4):
                nc.tensor.transpose(yt[:, P * he : P * he + P], ys[u][:, he, s, :], ident[:])
            yts[(u, s)] = yt

        def affine(u, s, lo=0, hi=T, on_vector=False):
            if u not in xnps:
                xnps[u] = work.tile([P, SLOTS, T], BF16, name="xnp")
            col = SLOTS * (u % NB) + s
            if on_vector:
                nc.vector.tensor_scalar(
                    out=xnps[u][:, s, lo:hi],
                    in0=yts[(u, s)][:, lo:hi],
                    scalar1=lnw[:, col : col + 1],
                    scalar2=lnb[:, col : col + 1],
                    op0=ALU.mult,
                    op1=ALU.add,
                )
            else:
                nc.scalar.activation(
                    out=xnps[u][:, s, lo:hi],
                    in_=yts[(u, s)][:, lo:hi],
                    func=ACT.Identity,
                    scale=lnw[:, col : col + 1],
                    bias=lnb[:, col : col + 1],
                )

        def regroup(u, q):
            if q == 0:
                grps[u] = work.tile([P, T, SLOTS], BF16, align_bytes=64, name="grp")
            nc.gpsimd.tensor_scalar(
                out=grps[u][:, 2 * P * q : 2 * P * q + 2 * P, :],
                in0=xnps[u][:, :, 2 * P * q : 2 * P * q + 2 * P].rearrange("p s t -> p t s"),
                scalar1=1.0,
                scalar2=0.0,
                op0=ALU.mult,
                op1=ALU.add,
            )

        def regroup_on_vector(u, h=None):
            fs = frames(h)
            if fs.start == 0:
                grps[u] = work.tile([P, T, SLOTS], BF16, align_bytes=64, name="grp")
            nc.vector.tensor_copy(
                out=grps[u][:, fs, :].rearrange("p (c i) s -> p c s i", i=4),
                in_=xnps[u][:, :, fs].rearrange("p s (c i) -> p c s i", i=4),
            )

        def quantise(u, h=None):
            fs = frames(h)
            if fs.start == 0:
                codes = work.tile([P, T], U32, align_bytes=64, name="codes")
                sc = work.tile([P, T], U8, align_bytes=64, name="sc")
                cds[u] = (codes, sc)
            codes, sc = cds[u]
            nc.vector.quantize_mx(
                out=codes[:, fs].bitcast(FP8X4),
                scales=sc[:, fs],
                in_=grps[u][:, fs, :].rearrange("p t s -> p (t s)"),
            )

        def multiply(u, h=None, busy=0):
            n = u % NB
            codes, sc = cds[u]
            if h is None:
                zo = psz.tile([P, 4 * EMB], F32, name="zo")
            else:
                zo = psy.tile([P, T], F32, tag="yt")
            keep_busy(zo[:], busy)
            for k, he in enumerate(blocks(h)):
                nc.tensor.matmul_mx(
                    out=zo[:, EMB * k : EMB * k + EMB],
                    lhsT=codes[:, P * he : P * he + P].bitcast(FP8X4),
                    lhsT_scale=sc[:, P * he : P * he + P],
                    rhs=wq["codes"][:, EMB * n : EMB * n + EMB].bitcast(FP8X4),
                    rhs_scale=wq["sc"][:, EMB * n : EMB * n + EMB],
                    start=True,
                    stop=True,
                )
            zos[(u, h)] = zo

        def finish(u, h=None):
            b, n = u // NB, u % NB
            hes = blocks(h)
            zs = zpool.tile([P, 4, EMB], F32, name="zs")
            nc.vector.tensor_tensor(
                out=zs[:, 0 : len(hes), :],
                in0=zos[(u, h)][:, 0 : len(hes) * EMB].rearrange("p (k m) -> p k m", m=EMB),
                in1=fcb[:, EMB * n : EMB * n + EMB].unsqueeze(1).to_broadcast([P, len(hes), EMB]),
                op=ALU.add,
            )
            nc.sync.dma_start(
                out=out[b, n].rearrange("(h p e) m -> p h (e m)", h=2, e=2)[:, hes[0] // 2 : hes[-1] // 2 + 1, :],
                in_=zs[:, 0 : len(hes), :].rearrange("p (h e) m -> p h (e m)", e=2),
            )

        for h in range(2):
            in_transposes(0, h)
            stats(0, h, 0)
            stats(0, h, 1)
            aggregate(0, h)
            root(0, 2 * h, 2 * h + 2)
            shift(0, 2 * h, 2 * h + 2)
            normalise(0, 2 * h)
            normalise(0, 2 * h + 1)
        load(AHEAD)
        gains()

        for i in range(-2, UNITS - 2):
            if ok(i - 1):
                regroup(i - 1, 0)
            if ok(i):
                affine(i, 2, 0, SHARE, on_vector=True)
            if i >= 0:
                normalise(i + 1, 0)
                normalise(i + 1, 1)
            if ok(i + 3):
                if ok(i + 3 + AHEAD):
                    load(i + 3 + AHEAD)
                in_transposes(i + 3, 0, busy=2 if i >= 2 else 0)
            if ok(i):
                affine(i, 0)
                affine(i, 1)
                back_transposes(i, 3)
            if ok(i - 3):
                multiply(i - 3, busy=1)
            if ok(i + 3):
                stats(i + 3, 0, 0)
                stats(i + 3, 0, 1)
            if i >= 0:
                normalise(i + 1, 2)
            if i >= -1:
                root(i + 2)
                shift(i + 2)
            if i in WEIGHT_ROUNDS:
                regroup_weights(*WEIGHT_ROUNDS[i])
            if ok(i - 1):
                regroup(i - 1, 1)
            if i >= 0:
                normalise(i + 1, 3)
            if ok(i + 3):
                in_transposes(i + 3, 1)
            if ok(i + 1):
                back_transposes(i + 1, 0)
            if ok(i + 3):
                stats(i + 3, 1, 0)
                stats(i + 3, 1, 1)
                aggregate(i + 3, 0)
            if ok(i - 3):
                finish(i - 3)
            if ok(i + 3):
                aggregate(i + 3, 1)
            if i in (0, 1):
                quantise_weights(i)
            if ok(i - 2):
                quantise(i - 2)
            if ok(i + 1):
                back_transposes(i + 1, 1)
            if ok(i):
                affine(i, 3)
                affine(i, 2, SHARE, T)
            if ok(i + 1):
                back_transposes(i + 1, 2)

        a, z = UNITS - 2, UNITS - 1
        quantise(a - 2)
        normalise(z, 0)
        normalise(z, 1)
        affine(a, 0)
        affine(a, 1)
        back_transposes(a, 3)
        multiply(a - 3)
        regroup_on_vector(a - 1)
        normalise(z, 2)
        normalise(z, 3)
        back_transposes(z, 0)
        back_transposes(z, 1)
        finish(a - 3)
        multiply(a - 2)
        quantise(a - 1)
        affine(a, 2)
        affine(a, 3)
        back_transposes(z, 2)
        finish(a - 2)
        multiply(a - 1)
        regroup_on_vector(a)
        affine(z, 0)
        affine(z, 1)
        back_transposes(z, 3)
        finish(a - 1)
        quantise(a)
        for lo, hi in ((0, T // 2), (T // 2, T)):
            affine(z, 2, lo, hi)
            affine(z, 3, lo, hi)
        multiply(a)
        regroup_on_vector(z, 0)
        regroup_on_vector(z, 1)
        quantise(z, 0)
        multiply(z, 0)
        quantise(z, 1)
        multiply(z, 1)
        finish(a)
        finish(z, 0)
        finish(z, 1)
